import numpy as np
import ml_dtypes


def mxq(x, axis, fmt="e4m3"):
    dtype, down = {"e4m3": (ml_dtypes.float8_e4m3fn, 7), "e5m2": (ml_dtypes.float8_e5m2, 14)}[fmt]
    v = np.moveaxis(np.asarray(x, np.float32).astype(ml_dtypes.bfloat16).astype(np.float64), axis, -1)
    blocks = v.reshape(v.shape[:-1] + (-1, 32))
    amax = np.abs(blocks).max(-1, keepdims=True)
    byte = np.maximum(np.where(amax > 0, np.frexp(amax)[1] - 1 + 127, 0) - down, 1)
    scale = np.exp2(byte - 127.0)
    codes = (blocks / scale).astype(np.float32).astype(dtype).astype(np.float64)
    return np.moveaxis((codes * scale).reshape(v.shape), -1, axis)


WIDE = False


def mx_kscale(k):
    if not WIDE:
        return np.ones(k)
    levels = np.array([10, -10, 5, -5, 0])
    a = np.random.permutation(np.resize(levels, k // 512 * 4)).reshape(k // 512, 4)
    idx = np.arange(k)
    return np.exp2(a[idx // 512, idx % 128 // 32])


BF16 = ml_dtypes.bfloat16


def bf(x):
    return np.asarray(x, np.float32).astype(BF16)


def f64(x):
    return np.asarray(x).astype(np.float64)


B, LQ, LS, D, SIM = 8, 128, 512, 1024, 1024
EPS = 1e-08


def l2norm(x):
    return x / (np.sqrt(np.sum(x * x, axis=-1, keepdims=True)) + EPS)


def setup_inputs():
    t = np.exp2(np.round(np.log2(mx_kscale(D)) / 2))
    c = np.sqrt(np.mean(t * t))
    return {"query": bf(np.random.standard_normal((B, LQ, D)) * 0.125 * t / c),
            "wcontext": bf(np.random.standard_normal((B, LQ, D)) * 3.6 / np.sqrt(LS) * t),
            "W": bf(np.random.standard_normal((SIM, D)) * 10.0 / np.sqrt(D) * (c * c) / (t * t)),
            "b": bf(np.random.standard_normal(SIM) * 0.05)}


def reference(query, wcontext, W, b):
    wn = l2norm(f64(wcontext))
    h = (f64(query) - wn) ** 2
    y = (mxq(h, 2, "e4m3") @ mxq(f64(W), 1, "e4m3").T) + f64(b)
    return l2norm(y)

@@ -1,0 +1,213 @@
+from contextlib import ExitStack
+
+import concourse.masks as masks
+import concourse.mybir as mybir
+
+F32 = mybir.dt.float32
+BF16 = mybir.dt.bfloat16
+U32 = mybir.dt.uint32
+U8 = mybir.dt.uint8
+FP8X4 = mybir.dt.float8_e4m3fn_x4
+ACT = mybir.ActivationFunctionType
+ALU = mybir.AluOpType
+
+P = 128
+PACK = 4
+K_PASS = P * PACK
+BATCH = 8
+D = 1024
+SIM = 1024
+PASSES = D // K_PASS
+N_TILE = 512
+HALVES = SIM // N_TILE
+W_CHUNKS = SIM // P
+CHUNKS_PER_HALF = W_CHUNKS // HALVES
+WORDS = D // 2
+EPS = 1e-08
+
+FLOPS = 2 * BATCH * P * D * SIM
+
+
+def tile_alignment_vector_pb_kernel(tc, query, wcontext, W, b, out):
+    nc = tc.nc
+    with ExitStack() as ctx:
+        keep = ctx.enter_context(tc.tile_pool(name="keep", bufs=1))
+        work = ctx.enter_context(tc.tile_pool(name="work", bufs=3))
+        psum_t = ctx.enter_context(tc.psum_pool(name="psum_t", bufs=4))
+        psum_acc = ctx.enter_context(tc.psum_pool(name="psum_acc", bufs=4))
+        ctx.enter_context(tc.manual_schedule())
+
+        ident = keep.tile([P, P], F32)
+        masks.make_identity(nc, ident[:])
+        ones = keep.tile([P, P], BF16)
+        nc.vector.memset(ones[:], 1.0)
+        b_row = keep.tile([P, SIM], BF16)
+        nc.vector.memset(b_row[:], 0.0)
+        one_col = keep.tile([P, 1], F32)
+        nc.vector.memset(one_col[:], 1.0)
+        sqrt_warm = keep.tile([P, 1], F32)
+        nc.scalar.activation(out=sqrt_warm[:], in_=one_col[:], func=ACT.Sqrt)
+
+        q_all = keep.tile([P, BATCH, D], BF16)
+        wc_all = keep.tile([P, BATCH, D], BF16)
+        w_rows = keep.tile([P, W_CHUNKS * D], BF16)
+        q_view = query.rearrange("b q d -> q b d")
+        wc_view = wcontext.rearrange("b q d -> q b d")
+        w_view = W.rearrange("(s p) d -> p s d", p=P)
+        out_view = out.rearrange("b q s -> q b s")
+
+        def load_rows(i):
+            nc.sync.dma_start(out=wc_all[:, i, :], in_=wc_view[:, i, :])
+            nc.sync.dma_start(out=q_all[:, i, :], in_=q_view[:, i, :])
+
+        def load_weights(half):
+            first = half * CHUNKS_PER_HALF
+            nc.sync.dma_start(
+                out=w_rows[:, first * D : (first + CHUNKS_PER_HALF) * D].rearrange(
+                    "p (s d) -> p s d", d=D
+                ),
+                in_=w_view[:, first : first + CHUNKS_PER_HALF, :],
+            )
+
+        load_rows(0)
+        nc.sync.dma_start(out=b_row[0:1, :], in_=b.unsqueeze(0))
+        load_weights(0)
+        load_rows(1)
+        load_weights(1)
+        for i in range(2, BATCH):
+            load_rows(i)
+
+        b_all = keep.tile([P, SIM], F32)
+        for half in range(HALVES):
+            cols = slice(half * N_TILE, (half + 1) * N_TILE)
+            b_bank = psum_t.tile([P, N_TILE], F32, tag="bank")
+            nc.tensor.matmul(out=b_bank[:], lhsT=ones[:], rhs=b_row[:, cols], start=True, stop=True)
+            nc.vector.tensor_copy(out=b_all[:, cols], in_=b_bank[:])
+
+        w_words = w_rows[:].bitcast(F32)
+        w_grouped = keep.tile([P, PASSES * SIM * PACK], BF16, align_bytes=64)
+        w_grouped_words = w_grouped[:].bitcast(F32).rearrange(
+            "p (g n u) -> p g n u", g=PASSES, u=2
+        )
+        w_codes = keep.tile([P, PASSES, SIM], U32, align_bytes=64)
+        w_scales = keep.tile([P, PASSES, SIM], U8, align_bytes=64)
+
+        def prepare_weights(half):
+            for s in range(half * CHUNKS_PER_HALF, (half + 1) * CHUNKS_PER_HALF):
+                w_bank = psum_t.tile([P, PASSES, 2, P], F32, tag="bank")
+                for g in range(PASSES):
+                    for u in range(2):
+                        first = s * WORDS + (2 * g + u) * P
+                        nc.tensor.transpose(
+                            w_bank[:, g, u, :], w_words[:, first : first + P], ident[:]
+                        )
+                dst = w_grouped_words[:, :, s * P : (s + 1) * P, :]
+                src = w_bank[:].rearrange("p g u n -> p g n u")
+                if s % 2 == 0:
+                    nc.scalar.copy(out=dst, in_=src)
+                else:
+                    nc.vector.tensor_copy(out=dst, in_=src)
+            for g in range(PASSES):
+                first = g * SIM + half * N_TILE
+                nc.vector.quantize_mx(
+                    out=w_codes[:, g, half * N_TILE : (half + 1) * N_TILE].bitcast(FP8X4),
+                    scales=w_scales[:, g, half * N_TILE : (half + 1) * N_TILE],
+                    in_=w_grouped[:, first * PACK : (first + N_TILE) * PACK],
+                )
+
+        wc_sumsq = keep.tile([P, BATCH], F32)
+        wc_norm = keep.tile([P, BATCH], F32)
+        wc_denom = keep.tile([P, BATCH], F32)
+        wc_scale = keep.tile([P, BATCH], F32)
+        y_sumsq = keep.tile([P, BATCH], F32)
+        y_norm = keep.tile([P, BATCH], F32)
+        y_denom = keep.tile([P, BATCH], F32)
+        y_scale = keep.tile([P, BATCH], F32)
+
+        def one_over_norm(rows, col, sumsq, norm, denom, scale):
+            squares = work.tile([P, D], BF16, tag="squares")
+            nc.scalar.activation(out=squares[:], in_=rows, func=ACT.Square, accum_out=sumsq[:, col])
+            nc.scalar.activation(out=norm[:, col], in_=sumsq[:, col], func=ACT.Sqrt)
+            nc.vector.tensor_scalar_add(out=denom[:, col], in0=norm[:, col], scalar1=EPS)
+            nc.vector.reciprocal(out=scale[:, col], in_=denom[:, col])
+
+        h_codes = keep.tile([P, BATCH, PASSES * P], U32, align_bytes=64)
+        h_scales = keep.tile([P, BATCH, PASSES * P], U8, align_bytes=64)
+
+        diffs = {}
+        ys = {}
+
+        def scale_and_subtract(i):
+            col = slice(i, i + 1)
+            one_over_norm(wc_all[:, i, :], col, wc_sumsq, wc_norm, wc_denom, wc_scale)
+            diff = work.tile([P, 2, WORDS], F32, tag="diff")
+            nc.vector.scalar_tensor_tensor(
+                out=diff[:],
+                in0=wc_all[:, i, :].rearrange("p (w e) -> p e w", e=2),
+                scalar=wc_scale[:, col],
+                in1=q_all[:, i, :].rearrange("p (w e) -> p e w", e=2),
+                op0=ALU.mult,
+                op1=ALU.subtract,
+            )
+            diffs[i] = diff
+
+        def square_and_quantise(i):
+            diff = diffs[i]
+            h_grouped = work.tile([P, PASSES, P, PACK], BF16, tag="h_grouped", align_bytes=64)
+            for g in range(PASSES):
+                d_bank = psum_t.tile([P, PACK, P], F32, tag="bank")
+                for u in range(2):
+                    for e in range(2):
+                        first = (2 * g + u) * P
+                        nc.tensor.transpose(
+                            d_bank[:, 2 * u + e, :], diff[:, e, first : first + P], ident[:]
+                        )
+                nc.scalar.activation(
+                    out=h_grouped[:, g, :, :],
+                    in_=d_bank[:].rearrange("p t r -> p r t"),
+                    func=ACT.Square,
+                )
+            nc.vector.quantize_mx(
+                out=h_codes[:, i, :].bitcast(FP8X4),
+                scales=h_scales[:, i, :],
+                in_=h_grouped[:].rearrange("p g r t -> p (g r t)"),
+            )
+
+        def multiply_and_add_bias(i):
+            y = work.tile([P, SIM], F32, tag="y")
+            for half in range(HALVES):
+                cols = slice(half * N_TILE, (half + 1) * N_TILE)
+                acc = psum_acc.tile([P, N_TILE], F32, tag="acc")
+                for g in range(PASSES):
+                    rows = slice(g * P, (g + 1) * P)
+                    nc.tensor.matmul_mx(
+                        out=acc[:],
+                        lhsT=h_codes[:, i, rows].bitcast(FP8X4),
+                        lhsT_scale=h_scales[:, i, rows],
+                        rhs=w_codes[:, g, cols].bitcast(FP8X4),
+                        rhs_scale=w_scales[:, g, cols],
+                        start=(g == 0),
+                        stop=(g == PASSES - 1),
+                    )
+                nc.vector.tensor_tensor(out=y[:, cols], in0=acc[:], in1=b_all[:, cols], op=ALU.add)
+            ys[i] = y
+
+        def normalise_and_store(i):
+            col = slice(i, i + 1)
+            y = ys[i]
+            one_over_norm(y[:], col, y_sumsq, y_norm, y_denom, y_scale)
+            nc.vector.tensor_scalar_mul(out=y[:], in0=y[:], scalar1=y_scale[:, col])
+            nc.sync.dma_start(out=out_view[:, i, :], in_=y[:])
+
+        stages = (
+            scale_and_subtract,
+            square_and_quantise,
+            multiply_and_add_bias,
+            normalise_and_store,
+        )
+        for n in range(BATCH + len(stages) - 1):
+            for lag, stage in enumerate(stages):
+                if 0 <= n - lag < BATCH:
+                    stage(n - lag)
+            if n < HALVES:
+                prepare_weights(n)

@@ -33,20 +33,20 @@ def tile_alignment_vector_pb_kernel(tc, query, wcontext, W, b, out):
     with ExitStack() as ctx:
         keep = ctx.enter_context(tc.tile_pool(name="keep", bufs=1))
         work = ctx.enter_context(tc.tile_pool(name="work", bufs=3))
-        psum_t = ctx.enter_context(tc.psum_pool(name="psum_t", bufs=4))
+        psum_d = ctx.enter_context(tc.psum_pool(name="psum_d", bufs=4))
         psum_acc = ctx.enter_context(tc.psum_pool(name="psum_acc", bufs=4))
         ctx.enter_context(tc.manual_schedule())
 
-        ident = keep.tile([P, P], F32)
-        masks.make_identity(nc, ident[:])
-        ones = keep.tile([P, P], BF16)
-        nc.vector.memset(ones[:], 1.0)
-        b_row = keep.tile([P, SIM], BF16)
-        nc.vector.memset(b_row[:], 0.0)
         one_col = keep.tile([P, 1], F32)
         nc.vector.memset(one_col[:], 1.0)
         sqrt_warm = keep.tile([P, 1], F32)
         nc.scalar.activation(out=sqrt_warm[:], in_=one_col[:], func=ACT.Sqrt)
+        ident = keep.tile([P, P], F32)
+        masks.make_identity(nc, ident[:])
+        b_row = keep.tile([P, SIM], BF16)
+        nc.vector.memset(b_row[:], 0.0)
+        ones = keep.tile([P, P], BF16)
+        nc.vector.memset(ones[:], 1.0)
 
         q_all = keep.tile([P, BATCH, D], BF16)
         wc_all = keep.tile([P, BATCH, D], BF16)
@@ -61,13 +61,11 @@ def tile_alignment_vector_pb_kernel(tc, query, wcontext, W, b, out):
             nc.sync.dma_start(out=q_all[:, i, :], in_=q_view[:, i, :])
 
         def load_weights(half):
-            first = half * CHUNKS_PER_HALF
-            nc.sync.dma_start(
-                out=w_rows[:, first * D : (first + CHUNKS_PER_HALF) * D].rearrange(
-                    "p (s d) -> p s d", d=D
-                ),
-                in_=w_view[:, first : first + CHUNKS_PER_HALF, :],
-            )
+            for first in range(half * CHUNKS_PER_HALF, (half + 1) * CHUNKS_PER_HALF, 2):
+                nc.sync.dma_start(
+                    out=w_rows[:, first * D : (first + 2) * D].rearrange("p (s d) -> p s d", d=D),
+                    in_=w_view[:, first : first + 2, :],
+                )
 
         load_rows(0)
         nc.sync.dma_start(out=b_row[0:1, :], in_=b.unsqueeze(0))
@@ -80,7 +78,7 @@ def tile_alignment_vector_pb_kernel(tc, query, wcontext, W, b, out):
         b_all = keep.tile([P, SIM], F32)
         for half in range(HALVES):
             cols = slice(half * N_TILE, (half + 1) * N_TILE)
-            b_bank = psum_t.tile([P, N_TILE], F32, tag="bank")
+            b_bank = psum_acc.tile([P, N_TILE], F32, tag="acc")
             nc.tensor.matmul(out=b_bank[:], lhsT=ones[:], rhs=b_row[:, cols], start=True, stop=True)
             nc.vector.tensor_copy(out=b_all[:, cols], in_=b_bank[:])
 
@@ -94,7 +92,7 @@ def tile_alignment_vector_pb_kernel(tc, query, wcontext, W, b, out):
 
         def prepare_weights(half):
             for s in range(half * CHUNKS_PER_HALF, (half + 1) * CHUNKS_PER_HALF):
-                w_bank = psum_t.tile([P, PASSES, 2, P], F32, tag="bank")
+                w_bank = psum_acc.tile([P, PASSES, 2, P], F32, tag="acc")
                 for g in range(PASSES):
                     for u in range(2):
                         first = s * WORDS + (2 * g + u) * P
@@ -115,66 +113,89 @@ def tile_alignment_vector_pb_kernel(tc, query, wcontext, W, b, out):
                     in_=w_grouped[:, first * PACK : (first + N_TILE) * PACK],
                 )
 
-        wc_sumsq = keep.tile([P, BATCH], F32)
-        wc_norm = keep.tile([P, BATCH], F32)
-        wc_denom = keep.tile([P, BATCH], F32)
-        wc_scale = keep.tile([P, BATCH], F32)
-        y_sumsq = keep.tile([P, BATCH], F32)
-        y_norm = keep.tile([P, BATCH], F32)
-        y_denom = keep.tile([P, BATCH], F32)
-        y_scale = keep.tile([P, BATCH], F32)
+        def norm_tiles(name):
+            sumsq = keep.tile([P, BATCH, 2], F32, name=name + "_sumsq")
+            nc.vector.memset(sumsq[:], EPS * EPS)
+            roots = keep.tile([P, BATCH, 2], F32, name=name + "_roots")
+            denom = keep.tile([P, BATCH], F32, name=name + "_denom")
+            scale = keep.tile([P, BATCH], F32, name=name + "_scale")
+            return sumsq, roots, denom, scale
 
-        def one_over_norm(rows, col, sumsq, norm, denom, scale):
+        wc_sumsq, wc_roots, wc_denom, wc_scale = norm_tiles("wc")
+        y_sumsq, y_roots, y_denom, y_scale = norm_tiles("y")
+
+        def sum_squares(rows, sumsq, i):
             squares = work.tile([P, D], BF16, tag="squares")
-            nc.scalar.activation(out=squares[:], in_=rows, func=ACT.Square, accum_out=sumsq[:, col])
-            nc.scalar.activation(out=norm[:, col], in_=sumsq[:, col], func=ACT.Sqrt)
-            nc.vector.tensor_scalar_add(out=denom[:, col], in0=norm[:, col], scalar1=EPS)
-            nc.vector.reciprocal(out=scale[:, col], in_=denom[:, col])
+            nc.scalar.activation(
+                out=squares[:], in_=rows, func=ACT.Square, accum_out=sumsq[:, i, 0:1]
+            )
+
+        def norm_plus_eps(sumsq, roots, denom, i):
+            nc.scalar.activation(
+                out=roots[:, i, :], in_=sumsq[:, i, :], func=ACT.Sqrt, accum_out=denom[:, i : i + 1]
+            )
+
+        def reciprocal(denom, scale, i):
+            nc.vector.reciprocal(out=scale[:, i : i + 1], in_=denom[:, i : i + 1])
 
         h_codes = keep.tile([P, BATCH, PASSES * P], U32, align_bytes=64)
         h_scales = keep.tile([P, BATCH, PASSES * P], U8, align_bytes=64)
-
         diffs = {}
+        d_banks = {}
+        h_groups = {}
+        accs = {}
         ys = {}
 
-        def scale_and_subtract(i):
-            col = slice(i, i + 1)
-            one_over_norm(wc_all[:, i, :], col, wc_sumsq, wc_norm, wc_denom, wc_scale)
+        def wc_sum_squares(i):
+            sum_squares(wc_all[:, i, :], wc_sumsq, i)
+
+        def wc_norm_plus_eps(i):
+            norm_plus_eps(wc_sumsq, wc_roots, wc_denom, i)
+
+        def wc_reciprocal(i):
+            reciprocal(wc_denom, wc_scale, i)
+
+        def subtract(i):
             diff = work.tile([P, 2, WORDS], F32, tag="diff")
             nc.vector.scalar_tensor_tensor(
                 out=diff[:],
                 in0=wc_all[:, i, :].rearrange("p (w e) -> p e w", e=2),
-                scalar=wc_scale[:, col],
+                scalar=wc_scale[:, i : i + 1],
                 in1=q_all[:, i, :].rearrange("p (w e) -> p e w", e=2),
                 op0=ALU.mult,
                 op1=ALU.subtract,
             )
             diffs[i] = diff
 
-        def square_and_quantise(i):
-            diff = diffs[i]
-            h_grouped = work.tile([P, PASSES, P, PACK], BF16, tag="h_grouped", align_bytes=64)
+        def transpose_diff(i):
             for g in range(PASSES):
-                d_bank = psum_t.tile([P, PACK, P], F32, tag="bank")
+                d_bank = psum_d.tile([P, PACK, P], F32, tag="d_bank")
                 for u in range(2):
                     for e in range(2):
                         first = (2 * g + u) * P
                         nc.tensor.transpose(
-                            d_bank[:, 2 * u + e, :], diff[:, e, first : first + P], ident[:]
+                            d_bank[:, 2 * u + e, :], diffs[i][:, e, first : first + P], ident[:]
                         )
+                d_banks[i, g] = d_bank
+
+        def square(i):
+            h_grouped = work.tile([P, PASSES, P, PACK], BF16, tag="h_grouped", align_bytes=64)
+            for g in range(PASSES):
                 nc.scalar.activation(
                     out=h_grouped[:, g, :, :],
-                    in_=d_bank[:].rearrange("p t r -> p r t"),
+                    in_=d_banks[i, g][:].rearrange("p t r -> p r t"),
                     func=ACT.Square,
                 )
+            h_groups[i] = h_grouped
+
+        def quantise(i):
             nc.vector.quantize_mx(
                 out=h_codes[:, i, :].bitcast(FP8X4),
                 scales=h_scales[:, i, :],
-                in_=h_grouped[:].rearrange("p g r t -> p (g r t)"),
+                in_=h_groups[i][:].rearrange("p g r t -> p (g r t)"),
             )
 
-        def multiply_and_add_bias(i):
-            y = work.tile([P, SIM], F32, tag="y")
+        def multiply(i):
             for half in range(HALVES):
                 cols = slice(half * N_TILE, (half + 1) * N_TILE)
                 acc = psum_acc.tile([P, N_TILE], F32, tag="acc")
@@ -189,25 +210,54 @@ def tile_alignment_vector_pb_kernel(tc, query, wcontext, W, b, out):
                         start=(g == 0),
                         stop=(g == PASSES - 1),
                     )
-                nc.vector.tensor_tensor(out=y[:, cols], in0=acc[:], in1=b_all[:, cols], op=ALU.add)
-            ys[i] = y
+                accs[i, half] = acc
 
-        def normalise_and_store(i):
-            col = slice(i, i + 1)
-            y = ys[i]
-            one_over_norm(y[:], col, y_sumsq, y_norm, y_denom, y_scale)
-            nc.vector.tensor_scalar_mul(out=y[:], in0=y[:], scalar1=y_scale[:, col])
-            nc.sync.dma_start(out=out_view[:, i, :], in_=y[:])
+        def add_bias(i, half):
+            if half == 0:
+                y = work.tile([P, SIM], F32, tag="y", bufs=6)
+                ys[i] = y
+            cols = slice(half * N_TILE, (half + 1) * N_TILE)
+            nc.vector.tensor_tensor(
+                out=ys[i][:, cols], in0=accs[i, half][:], in1=b_all[:, cols], op=ALU.add
+            )
 
-        stages = (
-            scale_and_subtract,
-            square_and_quantise,
-            multiply_and_add_bias,
-            normalise_and_store,
-        )
-        for n in range(BATCH + len(stages) - 1):
-            for lag, stage in enumerate(stages):
-                if 0 <= n - lag < BATCH:
-                    stage(n - lag)
+        def add_bias_first_half(i):
+            add_bias(i, 0)
+
+        def add_bias_second_half(i):
+            add_bias(i, 1)
+
+        def y_sum_squares(i):
+            sum_squares(ys[i][:], y_sumsq, i)
+
+        def y_norm_plus_eps(i):
+            norm_plus_eps(y_sumsq, y_roots, y_denom, i)
+
+        def y_reciprocal(i):
+            reciprocal(y_denom, y_scale, i)
+
+        def scale_and_store(i):
+            nc.vector.tensor_scalar_mul(out=ys[i][:], in0=ys[i][:], scalar1=y_scale[:, i : i + 1])
+            nc.sync.dma_start(out=out_view[:, i, :], in_=ys[i][:])
+
+        def at(step, i):
+            if 0 <= i < BATCH:
+                step(i)
+
+        for n in range(BATCH + 5):
+            at(wc_sum_squares, n)
+            at(add_bias_first_half, n - 3)
+            at(transpose_diff, n - 1)
+            at(square, n - 2)
+            at(quantise, n - 2)
+            at(multiply, n - 2)
+            at(y_norm_plus_eps, n - 5)
+            at(wc_norm_plus_eps, n)
+            at(y_reciprocal, n - 5)
+            at(wc_reciprocal, n)
+            at(add_bias_second_half, n - 3)
+            at(scale_and_store, n - 5)
+            at(subtract, n)
+            at(y_sum_squares, n - 4)
             if n < HALVES:
                 prepare_weights(n)

@@ -75,12 +75,14 @@ def tile_alignment_vector_pb_kernel(tc, query, wcontext, W, b, out):
         for i in range(2, BATCH):
             load_rows(i)
 
-        b_all = keep.tile([P, SIM], F32)
+        b_all = keep.tile([P, SIM], BF16)
+        b_bank = psum_acc.tile([P, SIM], BF16, tag="acc")
         for half in range(HALVES):
             cols = slice(half * N_TILE, (half + 1) * N_TILE)
-            b_bank = psum_acc.tile([P, N_TILE], F32, tag="acc")
-            nc.tensor.matmul(out=b_bank[:], lhsT=ones[:], rhs=b_row[:, cols], start=True, stop=True)
-            nc.vector.tensor_copy(out=b_all[:, cols], in_=b_bank[:])
+            nc.tensor.matmul(
+                out=b_bank[:, cols], lhsT=ones[:], rhs=b_row[:, cols], start=True, stop=True
+            )
+        nc.vector.tensor_copy(out=b_all[:], in_=b_bank[:])
 
         w_words = w_rows[:].bitcast(F32)
         w_grouped = keep.tile([P, PASSES * SIM * PACK], BF16, align_bytes=64)
@@ -237,8 +239,12 @@ def tile_alignment_vector_pb_kernel(tc, query, wcontext, W, b, out):
             reciprocal(y_denom, y_scale, i)
 
         def scale_and_store(i):
-            nc.vector.tensor_scalar_mul(out=ys[i][:], in0=ys[i][:], scalar1=y_scale[:, i : i + 1])
-            nc.sync.dma_start(out=out_view[:, i, :], in_=ys[i][:])
+            for half in range(HALVES):
+                cols = slice(half * N_TILE, (half + 1) * N_TILE)
+                nc.vector.tensor_scalar_mul(
+                    out=ys[i][:, cols], in0=ys[i][:, cols], scalar1=y_scale[:, i : i + 1]
+                )
+                nc.sync.dma_start(out=out_view[:, i, cols], in_=ys[i][:, cols])
 
         def at(step, i):
             if 0 <= i < BATCH:

@@ -239,6 +239,13 @@ def tile_alignment_vector_pb_kernel(tc, query, wcontext, W, b, out):
             reciprocal(y_denom, y_scale, i)
 
         def scale_and_store(i):
+            if i < BATCH - 1:
+                nc.gpsimd.tensor_scalar(
+                    out=ys[i][:], in0=ys[i][:], scalar1=y_scale[:, i : i + 1], scalar2=0.0,
+                    op0=ALU.mult, op1=ALU.add,
+                )
+                nc.sync.dma_start(out=out_view[:, i, :], in_=ys[i][:])
+                return
             for half in range(HALVES):
                 cols = slice(half * N_TILE, (half + 1) * N_TILE)
                 nc.vector.tensor_scalar_mul(
@@ -252,7 +259,6 @@ def tile_alignment_vector_pb_kernel(tc, query, wcontext, W, b, out):
 
         for n in range(BATCH + 5):
             at(wc_sum_squares, n)
-            at(add_bias_first_half, n - 3)
             at(transpose_diff, n - 1)
             at(square, n - 2)
             at(quantise, n - 2)
@@ -261,8 +267,9 @@ def tile_alignment_vector_pb_kernel(tc, query, wcontext, W, b, out):
             at(wc_norm_plus_eps, n)
             at(y_reciprocal, n - 5)
             at(wc_reciprocal, n)
-            at(add_bias_second_half, n - 3)
             at(scale_and_store, n - 5)
+            at(add_bias_first_half, n - 3)
+            at(add_bias_second_half, n - 3)
             at(subtract, n)
             at(y_sum_squares, n - 4)
             if n < HALVES:

@@ -24,6 +24,9 @@ W_CHUNKS = SIM // P
 CHUNKS_PER_HALF = W_CHUNKS // HALVES
 WORDS = D // 2
 EPS = 1e-08
+A_LEAD = 2
+BACK = 4
+SCALAR_W_CHUNKS = (1, 5)
 
 FLOPS = 2 * BATCH * P * D * SIM
 
@@ -56,33 +59,41 @@ def tile_alignment_vector_pb_kernel(tc, query, wcontext, W, b, out):
         w_view = W.rearrange("(s p) d -> p s d", p=P)
         out_view = out.rearrange("b q s -> q b s")
 
-        def load_rows(i):
+        def load_wc(i):
             nc.sync.dma_start(out=wc_all[:, i, :], in_=wc_view[:, i, :])
+
+        def load_q(i):
             nc.sync.dma_start(out=q_all[:, i, :], in_=q_view[:, i, :])
 
-        def load_weights(half):
-            for first in range(half * CHUNKS_PER_HALF, (half + 1) * CHUNKS_PER_HALF, 2):
-                nc.sync.dma_start(
-                    out=w_rows[:, first * D : (first + 2) * D].rearrange("p (s d) -> p s d", d=D),
-                    in_=w_view[:, first : first + 2, :],
-                )
+        def load_w(s):
+            nc.sync.dma_start(out=w_rows[:, s * D : (s + 1) * D], in_=w_view[:, s, :])
 
-        load_rows(0)
+        load_wc(0)
+        load_w(0)
         nc.sync.dma_start(out=b_row[0:1, :], in_=b.unsqueeze(0))
-        load_weights(0)
-        load_rows(1)
-        load_weights(1)
-        for i in range(2, BATCH):
-            load_rows(i)
+        load_q(0)
+        load_w(1)
+        for i in range(1, A_LEAD + 1):
+            load_wc(i)
+        for r in range(BATCH):
+            for s in (2 * r + 2, 2 * r + 3):
+                if s < W_CHUNKS:
+                    load_w(s)
+            if r + 1 < BATCH:
+                load_q(r + 1)
+            if r + A_LEAD + 1 < BATCH:
+                load_wc(r + A_LEAD + 1)
 
         b_all = keep.tile([P, SIM], BF16)
-        b_bank = psum_acc.tile([P, SIM], BF16, tag="acc")
-        for half in range(HALVES):
-            cols = slice(half * N_TILE, (half + 1) * N_TILE)
-            nc.tensor.matmul(
-                out=b_bank[:, cols], lhsT=ones[:], rhs=b_row[:, cols], start=True, stop=True
-            )
-        nc.vector.tensor_copy(out=b_all[:], in_=b_bank[:])
+
+        def spread_bias():
+            b_bank = psum_acc.tile([P, SIM], BF16, tag="acc")
+            for half in range(HALVES):
+                cols = slice(half * N_TILE, (half + 1) * N_TILE)
+                nc.tensor.matmul(
+                    out=b_bank[:, cols], lhsT=ones[:], rhs=b_row[:, cols], start=True, stop=True
+                )
+            nc.vector.tensor_copy(out=b_all[:], in_=b_bank[:])
 
         w_words = w_rows[:].bitcast(F32)
         w_grouped = keep.tile([P, PASSES * SIM * PACK], BF16, align_bytes=64)
@@ -92,21 +103,27 @@ def tile_alignment_vector_pb_kernel(tc, query, wcontext, W, b, out):
         w_codes = keep.tile([P, PASSES, SIM], U32, align_bytes=64)
         w_scales = keep.tile([P, PASSES, SIM], U8, align_bytes=64)
 
-        def prepare_weights(half):
-            for s in range(half * CHUNKS_PER_HALF, (half + 1) * CHUNKS_PER_HALF):
-                w_bank = psum_acc.tile([P, PASSES, 2, P], F32, tag="acc")
-                for g in range(PASSES):
-                    for u in range(2):
-                        first = s * WORDS + (2 * g + u) * P
-                        nc.tensor.transpose(
-                            w_bank[:, g, u, :], w_words[:, first : first + P], ident[:]
-                        )
-                dst = w_grouped_words[:, :, s * P : (s + 1) * P, :]
-                src = w_bank[:].rearrange("p g u n -> p g n u")
-                if s % 2 == 0:
-                    nc.scalar.copy(out=dst, in_=src)
-                else:
-                    nc.vector.tensor_copy(out=dst, in_=src)
+        w_banks = {}
+
+        def transpose_weights(s):
+            if s >= W_CHUNKS:
+                return
+            w_bank = psum_acc.tile([P, PASSES, 2, P], F32, tag="acc")
+            for g in range(PASSES):
+                for u in range(2):
+                    first = s * WORDS + (2 * g + u) * P
+                    nc.tensor.transpose(w_bank[:, g, u, :], w_words[:, first : first + P], ident[:])
+            w_banks[s] = w_bank
+
+        def regroup_weights(s):
+            dst = w_grouped_words[:, :, s * P : (s + 1) * P, :]
+            src = w_banks[s][:].rearrange("p g u n -> p g n u")
+            if s in SCALAR_W_CHUNKS:
+                nc.scalar.copy(out=dst, in_=src)
+            else:
+                nc.vector.tensor_copy(out=dst, in_=src)
+
+        def quantise_weights(half):
             for g in range(PASSES):
                 first = g * SIM + half * N_TILE
                 nc.vector.quantize_mx(
@@ -257,20 +274,34 @@ def tile_alignment_vector_pb_kernel(tc, query, wcontext, W, b, out):
             if 0 <= i < BATCH:
                 step(i)
 
-        for n in range(BATCH + 5):
-            at(wc_sum_squares, n)
-            at(transpose_diff, n - 1)
-            at(square, n - 2)
-            at(quantise, n - 2)
-            at(multiply, n - 2)
-            at(y_norm_plus_eps, n - 5)
-            at(wc_norm_plus_eps, n)
-            at(y_reciprocal, n - 5)
-            at(wc_reciprocal, n)
-            at(scale_and_store, n - 5)
-            at(add_bias_first_half, n - 3)
-            at(add_bias_second_half, n - 3)
-            at(subtract, n)
-            at(y_sum_squares, n - 4)
-            if n < HALVES:
-                prepare_weights(n)
+        def norm_of_wc(i):
+            wc_sum_squares(i)
+            wc_norm_plus_eps(i)
+
+        for i in range(A_LEAD):
+            norm_of_wc(i)
+        transpose_weights(0)
+        spread_bias()
+        transpose_weights(1)
+        wc_reciprocal(0)
+        for r in range(BATCH + BACK + 3):
+            at(subtract, r)
+            at(transpose_diff, r)
+            at(y_reciprocal, r - BACK - 2)
+            at(scale_and_store, r - BACK - 2)
+            at(add_bias_first_half, r - BACK)
+            at(add_bias_second_half, r - BACK)
+            if r < W_CHUNKS // 2:
+                regroup_weights(2 * r)
+                regroup_weights(2 * r + 1)
+                transpose_weights(2 * r + 2)
+                transpose_weights(2 * r + 3)
+                if r % 2 == 1:
+                    quantise_weights(r // 2)
+            at(wc_reciprocal, r + 1)
+            at(square, r - 1)
+            at(y_sum_squares, r - BACK - 1)
+            at(y_norm_plus_eps, r - BACK - 1)
+            at(norm_of_wc, r + A_LEAD)
+            at(quantise, r - 1)
+            at(multiply, r + 1 - BACK)

@@ -25,6 +25,7 @@ CHUNKS_PER_HALF = W_CHUNKS // HALVES
 WORDS = D // 2
 EPS = 1e-08
 A_LEAD = 2
+VECTOR_SCALES_LAST = 2
 BACK = 4
 SCALAR_W_CHUNKS = (1, 5)
 
@@ -197,15 +198,23 @@ def tile_alignment_vector_pb_kernel(tc, query, wcontext, W, b, out):
                         )
                 d_banks[i, g] = d_bank
 
-        def square(i):
-            h_grouped = work.tile([P, PASSES, P, PACK], BF16, tag="h_grouped", align_bytes=64)
-            for g in range(PASSES):
-                nc.scalar.activation(
-                    out=h_grouped[:, g, :, :],
-                    in_=d_banks[i, g][:].rearrange("p t r -> p r t"),
-                    func=ACT.Square,
+        def square(i, g):
+            if g == 0:
+                h_grouped = work.tile(
+                    [P, PASSES, P, PACK], BF16, tag="h_grouped", align_bytes=64, bufs=4
                 )
-            h_groups[i] = h_grouped
+                h_groups[i] = h_grouped
+            nc.scalar.activation(
+                out=h_groups[i][:, g, :, :],
+                in_=d_banks[i, g][:].rearrange("p t r -> p r t"),
+                func=ACT.Square,
+            )
+
+        def square_first_pass(i):
+            square(i, 0)
+
+        def square_second_pass(i):
+            square(i, 1)
 
         def quantise(i):
             nc.vector.quantize_mx(
@@ -256,7 +265,7 @@ def tile_alignment_vector_pb_kernel(tc, query, wcontext, W, b, out):
             reciprocal(y_denom, y_scale, i)
 
         def scale_and_store(i):
-            if i < BATCH - 1:
+            if i < BATCH - VECTOR_SCALES_LAST:
                 nc.gpsimd.tensor_scalar(
                     out=ys[i][:], in0=ys[i][:], scalar1=y_scale[:, i : i + 1], scalar2=0.0,
                     op0=ALU.mult, op1=ALU.add,
@@ -274,12 +283,9 @@ def tile_alignment_vector_pb_kernel(tc, query, wcontext, W, b, out):
             if 0 <= i < BATCH:
                 step(i)
 
-        def norm_of_wc(i):
-            wc_sum_squares(i)
-            wc_norm_plus_eps(i)
-
-        for i in range(A_LEAD):
-            norm_of_wc(i)
+        wc_sum_squares(0)
+        wc_norm_plus_eps(0)
+        wc_sum_squares(1)
         transpose_weights(0)
         spread_bias()
         transpose_weights(1)
@@ -287,6 +293,12 @@ def tile_alignment_vector_pb_kernel(tc, query, wcontext, W, b, out):
         for r in range(BATCH + BACK + 3):
             at(subtract, r)
             at(transpose_diff, r)
+            at(square_first_pass, r - 1)
+            at(wc_norm_plus_eps, r + 1)
+            at(square_second_pass, r - 1)
+            at(y_sum_squares, r - BACK - 1)
+            at(wc_sum_squares, r + A_LEAD)
+            at(y_norm_plus_eps, r - BACK - 1)
             at(y_reciprocal, r - BACK - 2)
             at(scale_and_store, r - BACK - 2)
             at(add_bias_first_half, r - BACK)
@@ -299,9 +311,5 @@ def tile_alignment_vector_pb_kernel(tc, query, wcontext, W, b, out):
                 if r % 2 == 1:
                     quantise_weights(r // 2)
             at(wc_reciprocal, r + 1)
-            at(square, r - 1)
-            at(y_sum_squares, r - BACK - 1)
-            at(y_norm_plus_eps, r - BACK - 1)
-            at(norm_of_wc, r + A_LEAD)
             at(quantise, r - 1)
             at(multiply, r + 1 - BACK)

@@ -290,26 +290,28 @@ def tile_alignment_vector_pb_kernel(tc, query, wcontext, W, b, out):
         spread_bias()
         transpose_weights(1)
         wc_reciprocal(0)
+        regroup_weights(0)
         for r in range(BATCH + BACK + 3):
             at(subtract, r)
             at(transpose_diff, r)
             at(square_first_pass, r - 1)
             at(wc_norm_plus_eps, r + 1)
-            at(square_second_pass, r - 1)
             at(y_sum_squares, r - BACK - 1)
-            at(wc_sum_squares, r + A_LEAD)
+            at(square_second_pass, r - 1)
             at(y_norm_plus_eps, r - BACK - 1)
+            at(wc_sum_squares, r + A_LEAD)
             at(y_reciprocal, r - BACK - 2)
             at(scale_and_store, r - BACK - 2)
             at(add_bias_first_half, r - BACK)
             at(add_bias_second_half, r - BACK)
             if r < W_CHUNKS // 2:
-                regroup_weights(2 * r)
+                if r > 0:
+                    regroup_weights(2 * r)
                 regroup_weights(2 * r + 1)
                 transpose_weights(2 * r + 2)
                 transpose_weights(2 * r + 3)
-                if r % 2 == 1:
-                    quantise_weights(r // 2)
             at(wc_reciprocal, r + 1)
-            at(quantise, r - 1)
+            at(quantise, r - 2)
+            if r < W_CHUNKS // 2 and r % 2 == 1:
+                quantise_weights(r // 2)
             at(multiply, r + 1 - BACK)

@@ -25,7 +25,7 @@ CHUNKS_PER_HALF = W_CHUNKS // HALVES
 WORDS = D // 2
 EPS = 1e-08
 A_LEAD = 2
-VECTOR_SCALES_LAST = 2
+VECTOR_SCALES_LAST = 3
 BACK = 4
 SCALAR_W_CHUNKS = (1, 5)
 
@@ -69,8 +69,8 @@ def tile_alignment_vector_pb_kernel(tc, query, wcontext, W, b, out):
         def load_w(s):
             nc.sync.dma_start(out=w_rows[:, s * D : (s + 1) * D], in_=w_view[:, s, :])
 
-        load_wc(0)
         load_w(0)
+        load_wc(0)
         nc.sync.dma_start(out=b_row[0:1, :], in_=b.unsqueeze(0))
         load_q(0)
         load_w(1)
@@ -87,14 +87,14 @@ def tile_alignment_vector_pb_kernel(tc, query, wcontext, W, b, out):
 
         b_all = keep.tile([P, SIM], BF16)
 
+        b_bank = psum_acc.tile([P, SIM], BF16, tag="acc")
+
         def spread_bias():
-            b_bank = psum_acc.tile([P, SIM], BF16, tag="acc")
             for half in range(HALVES):
                 cols = slice(half * N_TILE, (half + 1) * N_TILE)
                 nc.tensor.matmul(
                     out=b_bank[:, cols], lhsT=ones[:], rhs=b_row[:, cols], start=True, stop=True
                 )
-            nc.vector.tensor_copy(out=b_all[:], in_=b_bank[:])
 
         w_words = w_rows[:].bitcast(F32)
         w_grouped = keep.tile([P, PASSES * SIM * PACK], BF16, align_bytes=64)
@@ -289,8 +289,9 @@ def tile_alignment_vector_pb_kernel(tc, query, wcontext, W, b, out):
         transpose_weights(0)
         spread_bias()
         transpose_weights(1)
-        wc_reciprocal(0)
         regroup_weights(0)
+        wc_reciprocal(0)
+        nc.vector.tensor_copy(out=b_all[:], in_=b_bank[:])
         for r in range(BATCH + BACK + 3):
             at(subtract, r)
             at(transpose_diff, r)
@@ -300,10 +301,19 @@ def tile_alignment_vector_pb_kernel(tc, query, wcontext, W, b, out):
             at(square_second_pass, r - 1)
             at(y_norm_plus_eps, r - BACK - 1)
             at(wc_sum_squares, r + A_LEAD)
-            at(y_reciprocal, r - BACK - 2)
-            at(scale_and_store, r - BACK - 2)
-            at(add_bias_first_half, r - BACK)
+            if r > BATCH:
+                at(add_bias_first_half, r - BACK)
+                at(quantise, r - 2)
+            scaled_by_vector = r - BACK - 2 >= BATCH - VECTOR_SCALES_LAST
+            if not scaled_by_vector:
+                at(y_reciprocal, r - BACK - 2)
+                at(scale_and_store, r - BACK - 2)
+            if r <= BATCH:
+                at(add_bias_first_half, r - BACK)
             at(add_bias_second_half, r - BACK)
+            if scaled_by_vector:
+                at(y_reciprocal, r - BACK - 2)
+                at(scale_and_store, r - BACK - 2)
             if r < W_CHUNKS // 2:
                 if r > 0:
                     regroup_weights(2 * r)
@@ -311,7 +321,8 @@ def tile_alignment_vector_pb_kernel(tc, query, wcontext, W, b, out):
                 transpose_weights(2 * r + 2)
                 transpose_weights(2 * r + 3)
             at(wc_reciprocal, r + 1)
-            at(quantise, r - 2)
+            if r <= BATCH:
+                at(quantise, r - 2)
             if r < W_CHUNKS // 2 and r % 2 == 1:
                 quantise_weights(r // 2)
             at(multiply, r + 1 - BACK)

from contextlib import ExitStack

import concourse.masks as masks
import concourse.mybir as mybir

F32 = mybir.dt.float32
BF16 = mybir.dt.bfloat16
U32 = mybir.dt.uint32
U8 = mybir.dt.uint8
FP8X4 = mybir.dt.float8_e4m3fn_x4
ACT = mybir.ActivationFunctionType
ALU = mybir.AluOpType

P = 128
PACK = 4
K_PASS = P * PACK
BATCH = 8
D = 1024
SIM = 1024
PASSES = D // K_PASS
N_TILE = 512
HALVES = SIM // N_TILE
W_CHUNKS = SIM // P
CHUNKS_PER_HALF = W_CHUNKS // HALVES
WORDS = D // 2
EPS = 1e-08
A_LEAD = 2
VECTOR_SCALES_LAST = 3
BACK = 4
SCALAR_W_CHUNKS = (1, 5)

FLOPS = 2 * BATCH * P * D * SIM


def tile_alignment_vector_pb_kernel(tc, query, wcontext, W, b, out):
    nc = tc.nc
    with ExitStack() as ctx:
        keep = ctx.enter_context(tc.tile_pool(name="keep", bufs=1))
        work = ctx.enter_context(tc.tile_pool(name="work", bufs=3))
        psum_d = ctx.enter_context(tc.psum_pool(name="psum_d", bufs=4))
        psum_acc = ctx.enter_context(tc.psum_pool(name="psum_acc", bufs=4))
        ctx.enter_context(tc.manual_schedule())

        one_col = keep.tile([P, 1], F32)
        nc.vector.memset(one_col[:], 1.0)
        sqrt_warm = keep.tile([P, 1], F32)
        nc.scalar.activation(out=sqrt_warm[:], in_=one_col[:], func=ACT.Sqrt)
        ident = keep.tile([P, P], F32)
        masks.make_identity(nc, ident[:])
        b_row = keep.tile([P, SIM], BF16)
        nc.vector.memset(b_row[:], 0.0)
        ones = keep.tile([P, P], BF16)
        nc.vector.memset(ones[:], 1.0)

        q_all = keep.tile([P, BATCH, D], BF16)
        wc_all = keep.tile([P, BATCH, D], BF16)
        w_rows = keep.tile([P, W_CHUNKS * D], BF16)
        q_view = query.rearrange("b q d -> q b d")
        wc_view = wcontext.rearrange("b q d -> q b d")
        w_view = W.rearrange("(s p) d -> p s d", p=P)
        out_view = out.rearrange("b q s -> q b s")

        def load_wc(i):
            nc.sync.dma_start(out=wc_all[:, i, :], in_=wc_view[:, i, :])

        def load_q(i):
            nc.sync.dma_start(out=q_all[:, i, :], in_=q_view[:, i, :])

        def load_w(s):
            nc.sync.dma_start(out=w_rows[:, s * D : (s + 1) * D], in_=w_view[:, s, :])

        load_w(0)
        load_wc(0)
        nc.sync.dma_start(out=b_row[0:1, :], in_=b.unsqueeze(0))
        load_q(0)
        load_w(1)
        for i in range(1, A_LEAD + 1):
            load_wc(i)
        for r in range(BATCH):
            for s in (2 * r + 2, 2 * r + 3):
                if s < W_CHUNKS:
                    load_w(s)
            if r + 1 < BATCH:
                load_q(r + 1)
            if r + A_LEAD + 1 < BATCH:
                load_wc(r + A_LEAD + 1)

        b_all = keep.tile([P, SIM], BF16)

        b_bank = psum_acc.tile([P, SIM], BF16, tag="acc")

        def spread_bias():
            for half in range(HALVES):
                cols = slice(half * N_TILE, (half + 1) * N_TILE)
                nc.tensor.matmul(
                    out=b_bank[:, cols], lhsT=ones[:], rhs=b_row[:, cols], start=True, stop=True
                )

        w_words = w_rows[:].bitcast(F32)
        w_grouped = keep.tile([P, PASSES * SIM * PACK], BF16, align_bytes=64)
        w_grouped_words = w_grouped[:].bitcast(F32).rearrange(
            "p (g n u) -> p g n u", g=PASSES, u=2
        )
        w_codes = keep.tile([P, PASSES, SIM], U32, align_bytes=64)
        w_scales = keep.tile([P, PASSES, SIM], U8, align_bytes=64)

        w_banks = {}

        def transpose_weights(s):
            if s >= W_CHUNKS:
                return
            w_bank = psum_acc.tile([P, PASSES, 2, P], F32, tag="acc")
            for g in range(PASSES):
                for u in range(2):
                    first = s * WORDS + (2 * g + u) * P
                    nc.tensor.transpose(w_bank[:, g, u, :], w_words[:, first : first + P], ident[:])
            w_banks[s] = w_bank

        def regroup_weights(s):
            dst = w_grouped_words[:, :, s * P : (s + 1) * P, :]
            src = w_banks[s][:].rearrange("p g u n -> p g n u")
            if s in SCALAR_W_CHUNKS:
                nc.scalar.copy(out=dst, in_=src)
            else:
                nc.vector.tensor_copy(out=dst, in_=src)

        def quantise_weights(half):
            for g in range(PASSES):
                first = g * SIM + half * N_TILE
                nc.vector.quantize_mx(
                    out=w_codes[:, g, half * N_TILE : (half + 1) * N_TILE].bitcast(FP8X4),
                    scales=w_scales[:, g, half * N_TILE : (half + 1) * N_TILE],
                    in_=w_grouped[:, first * PACK : (first + N_TILE) * PACK],
                )

        def norm_tiles(name):
            sumsq = keep.tile([P, BATCH, 2], F32, name=name + "_sumsq")
            nc.vector.memset(sumsq[:], EPS * EPS)
            roots = keep.tile([P, BATCH, 2], F32, name=name + "_roots")
            denom = keep.tile([P, BATCH], F32, name=name + "_denom")
            scale = keep.tile([P, BATCH], F32, name=name + "_scale")
            return sumsq, roots, denom, scale

        wc_sumsq, wc_roots, wc_denom, wc_scale = norm_tiles("wc")
        y_sumsq, y_roots, y_denom, y_scale = norm_tiles("y")

        def sum_squares(rows, sumsq, i):
            squares = work.tile([P, D], BF16, tag="squares")
            nc.scalar.activation(
                out=squares[:], in_=rows, func=ACT.Square, accum_out=sumsq[:, i, 0:1]
            )

        def norm_plus_eps(sumsq, roots, denom, i):
            nc.scalar.activation(
                out=roots[:, i, :], in_=sumsq[:, i, :], func=ACT.Sqrt, accum_out=denom[:, i : i + 1]
            )

        def reciprocal(denom, scale, i):
            nc.vector.reciprocal(out=scale[:, i : i + 1], in_=denom[:, i : i + 1])

        h_codes = keep.tile([P, BATCH, PASSES * P], U32, align_bytes=64)
        h_scales = keep.tile([P, BATCH, PASSES * P], U8, align_bytes=64)
        diffs = {}
        d_banks = {}
        h_groups = {}
        accs = {}
        ys = {}

        def wc_sum_squares(i):
            sum_squares(wc_all[:, i, :], wc_sumsq, i)

        def wc_norm_plus_eps(i):
            norm_plus_eps(wc_sumsq, wc_roots, wc_denom, i)

        def wc_reciprocal(i):
            reciprocal(wc_denom, wc_scale, i)

        def subtract(i):
            diff = work.tile([P, 2, WORDS], F32, tag="diff")
            nc.vector.scalar_tensor_tensor(
                out=diff[:],
                in0=wc_all[:, i, :].rearrange("p (w e) -> p e w", e=2),
                scalar=wc_scale[:, i : i + 1],
                in1=q_all[:, i, :].rearrange("p (w e) -> p e w", e=2),
                op0=ALU.mult,
                op1=ALU.subtract,
            )
            diffs[i] = diff

        def transpose_diff(i):
            for g in range(PASSES):
                d_bank = psum_d.tile([P, PACK, P], F32, tag="d_bank")
                for u in range(2):
                    for e in range(2):
                        first = (2 * g + u) * P
                        nc.tensor.transpose(
                            d_bank[:, 2 * u + e, :], diffs[i][:, e, first : first + P], ident[:]
                        )
                d_banks[i, g] = d_bank

        def square(i, g):
            if g == 0:
                h_grouped = work.tile(
                    [P, PASSES, P, PACK], BF16, tag="h_grouped", align_bytes=64, bufs=4
                )
                h_groups[i] = h_grouped
            nc.scalar.activation(
                out=h_groups[i][:, g, :, :],
                in_=d_banks[i, g][:].rearrange("p t r -> p r t"),
                func=ACT.Square,
            )

        def square_first_pass(i):
            square(i, 0)

        def square_second_pass(i):
            square(i, 1)

        def quantise(i):
            nc.vector.quantize_mx(
                out=h_codes[:, i, :].bitcast(FP8X4),
                scales=h_scales[:, i, :],
                in_=h_groups[i][:].rearrange("p g r t -> p (g r t)"),
            )

        def multiply(i):
            for half in range(HALVES):
                cols = slice(half * N_TILE, (half + 1) * N_TILE)
                acc = psum_acc.tile([P, N_TILE], F32, tag="acc")
                for g in range(PASSES):
                    rows = slice(g * P, (g + 1) * P)
                    nc.tensor.matmul_mx(
                        out=acc[:],
                        lhsT=h_codes[:, i, rows].bitcast(FP8X4),
                        lhsT_scale=h_scales[:, i, rows],
                        rhs=w_codes[:, g, cols].bitcast(FP8X4),
                        rhs_scale=w_scales[:, g, cols],
                        start=(g == 0),
                        stop=(g == PASSES - 1),
                    )
                accs[i, half] = acc

        def add_bias(i, half):
            if half == 0:
                y = work.tile([P, SIM], F32, tag="y", bufs=6)
                ys[i] = y
            cols = slice(half * N_TILE, (half + 1) * N_TILE)
            nc.vector.tensor_tensor(
                out=ys[i][:, cols], in0=accs[i, half][:], in1=b_all[:, cols], op=ALU.add
            )

        def add_bias_first_half(i):
            add_bias(i, 0)

        def add_bias_second_half(i):
            add_bias(i, 1)

        def y_sum_squares(i):
            sum_squares(ys[i][:], y_sumsq, i)

        def y_norm_plus_eps(i):
            norm_plus_eps(y_sumsq, y_roots, y_denom, i)

        def y_reciprocal(i):
            reciprocal(y_denom, y_scale, i)

        def scale_and_store(i):
            if i < BATCH - VECTOR_SCALES_LAST:
                nc.gpsimd.tensor_scalar(
                    out=ys[i][:], in0=ys[i][:], scalar1=y_scale[:, i : i + 1], scalar2=0.0,
                    op0=ALU.mult, op1=ALU.add,
                )
                nc.sync.dma_start(out=out_view[:, i, :], in_=ys[i][:])
                return
            for half in range(HALVES):
                cols = slice(half * N_TILE, (half + 1) * N_TILE)
                nc.vector.tensor_scalar_mul(
                    out=ys[i][:, cols], in0=ys[i][:, cols], scalar1=y_scale[:, i : i + 1]
                )
                nc.sync.dma_start(out=out_view[:, i, cols], in_=ys[i][:, cols])

        def at(step, i):
            if 0 <= i < BATCH:
                step(i)

        wc_sum_squares(0)
        wc_norm_plus_eps(0)
        wc_sum_squares(1)
        transpose_weights(0)
        spread_bias()
        transpose_weights(1)
        regroup_weights(0)
        wc_reciprocal(0)
        nc.vector.tensor_copy(out=b_all[:], in_=b_bank[:])
        for r in range(BATCH + BACK + 3):
            at(subtract, r)
            at(transpose_diff, r)
            at(square_first_pass, r - 1)
            at(wc_norm_plus_eps, r + 1)
            at(y_sum_squares, r - BACK - 1)
            at(square_second_pass, r - 1)
            at(y_norm_plus_eps, r - BACK - 1)
            at(wc_sum_squares, r + A_LEAD)
            if r > BATCH:
                at(add_bias_first_half, r - BACK)
                at(quantise, r - 2)
            scaled_by_vector = r - BACK - 2 >= BATCH - VECTOR_SCALES_LAST
            if not scaled_by_vector:
                at(y_reciprocal, r - BACK - 2)
                at(scale_and_store, r - BACK - 2)
            if r <= BATCH:
                at(add_bias_first_half, r - BACK)
            at(add_bias_second_half, r - BACK)
            if scaled_by_vector:
                at(y_reciprocal, r - BACK - 2)
                at(scale_and_store, r - BACK - 2)
            if r < W_CHUNKS // 2:
                if r > 0:
                    regroup_weights(2 * r)
                regroup_weights(2 * r + 1)
                transpose_weights(2 * r + 2)
                transpose_weights(2 * r + 3)
            at(wc_reciprocal, r + 1)
            if r <= BATCH:
                at(quantise, r - 2)
            if r < W_CHUNKS // 2 and r % 2 == 1:
                quantise_weights(r // 2)
            at(multiply, r + 1 - BACK)
